import numpy as np
import ml_dtypes


def mxq(x, axis, fmt="e4m3"):
    dtype, down = {"e4m3": (ml_dtypes.float8_e4m3fn, 7), "e5m2": (ml_dtypes.float8_e5m2, 14)}[fmt]
    v = np.moveaxis(np.asarray(x, np.float32).astype(ml_dtypes.bfloat16).astype(np.float64), axis, -1)
    blocks = v.reshape(v.shape[:-1] + (-1, 32))
    amax = np.abs(blocks).max(-1, keepdims=True)
    byte = np.maximum(np.where(amax > 0, np.frexp(amax)[1] - 1 + 127, 0) - down, 1)
    scale = np.exp2(byte - 127.0)
    codes = (blocks / scale).astype(np.float32).astype(dtype).astype(np.float64)
    return np.moveaxis((codes * scale).reshape(v.shape), -1, axis)


WIDE = False


def mx_kscale(k):
    if not WIDE:
        return np.ones(k)
    levels = np.array([10, -10, 5, -5, 0])
    if k % 512:
        return np.exp2(np.random.permutation(np.resize(levels, k // 32))).repeat(32)
    a = np.empty((k // 512, 16))
    for p in range(k // 512):
        a[p, :8] = np.random.permutation(np.resize(levels, 8))
        for g in range(8):
            far = levels[np.abs(levels - a[p, g]) >= 10]
            a[p, g + 8] = far[np.random.randint(len(far))]
    return np.exp2(a.ravel()).repeat(32)


BF16 = ml_dtypes.bfloat16


def bf(x):
    return np.asarray(x, np.float32).astype(BF16)


def f64(x):
    return np.asarray(x).astype(np.float64)


B, T, HID, H, NOPE, ROPE, VD, KV_LORA = 4, 2048, 512, 4, 64, 64, 128, 512
QK = NOPE + ROPE
HALF = ROPE // 2


def rope(x, cos, sin):
    c = cos[None, :, None, :]
    s = sin[None, :, None, :]
    x1, x2 = x[..., 0::2], x[..., 1::2]
    o1 = x1 * c - x2 * s
    o2 = x1 * s + x2 * c
    return np.stack([o1, o2], axis=-1).reshape(x.shape)


def setup_inputs():
    s = mx_kscale(HID)
    ang = np.random.uniform(-np.pi, np.pi, (T, HALF))
    return {"hidden_states": bf(np.random.standard_normal((B, T, HID)) * s),
            "rope_cos": bf(np.cos(ang)), "rope_sin": bf(np.sin(ang)),
            "Wq": bf(np.random.standard_normal((HID, H * QK)) / np.sqrt(HID) / s[:, None])}


def reference(hidden_states, rope_cos, rope_sin, Wq):
    q = (mxq(f64(hidden_states), 2, "e4m3") @ mxq(f64(Wq), 0, "e4m3")).reshape(B, T, H, QK)
    q_nope, q_rope = q[..., :NOPE], q[..., NOPE:]
    q_rope = rope(q_rope, f64(rope_cos), f64(rope_sin))
    return np.concatenate([q_nope, q_rope], axis=-1)

@@ -1,0 +1,176 @@
+from contextlib import ExitStack
+
+import concourse.mybir as mybir
+from concourse.masks import make_identity
+
+F32 = mybir.dt.float32
+BF16 = mybir.dt.bfloat16
+U32 = mybir.dt.uint32
+U8 = mybir.dt.uint8
+FP8X4 = mybir.dt.float8_e4m3fn_x4
+MULT = mybir.AluOpType.mult
+ADD = mybir.AluOpType.add
+
+P = 128
+PACK = 4
+BATCH, TOKENS, HID = 4, 2048, 512
+HEADS, HEAD_DIM = 4, 128
+NOPE = 64
+PAIRS = 32
+COLS = HEADS * HEAD_DIM
+PLAIN_COLS = HEADS * NOPE
+PLANE = HEADS * PAIRS
+TILES_PER_BATCH = TOKENS // P
+STEP_TILES = 2
+STEPS_PER_BATCH = TILES_PER_BATCH // STEP_TILES
+STEPS = BATCH * STEPS_PER_BATCH
+LOAD_TILES = 4
+STEPS_PER_LOAD = LOAD_TILES // STEP_TILES
+LOADS = BATCH * TILES_PER_BATCH // LOAD_TILES
+WORDS = HID // 2
+
+FLOPS = 2 * BATCH * TOKENS * HID * COLS
+
+
+def tile_multilatentattention_pb_t_kernel(tc, hidden_states, rope_cos, rope_sin, Wq, out):
+    nc = tc.nc
+    x_view = hidden_states.rearrange("b (p j) k -> b p j k", p=P)
+    out_view = out.rearrange("b (p j) h d -> b p j (h d)", p=P)
+
+    with ExitStack() as ctx:
+        const = ctx.enter_context(tc.tile_pool(name="const", bufs=1))
+        x_pool = ctx.enter_context(tc.tile_pool(name="x", bufs=LOADS))
+        grouped_pool = ctx.enter_context(tc.tile_pool(name="grouped", bufs=3))
+        mx_pool = ctx.enter_context(tc.tile_pool(name="mx", bufs=3))
+        product_pool = ctx.enter_context(tc.tile_pool(name="product", bufs=3))
+        out_pool = ctx.enter_context(tc.tile_pool(name="result", bufs=8))
+        xt_pool = ctx.enter_context(tc.psum_pool(name="xt", bufs=2))
+        plain_pool = ctx.enter_context(tc.psum_pool(name="plain", bufs=3))
+        rope_pool = ctx.enter_context(tc.psum_pool(name="rope", bufs=3))
+
+        def load_tokens(load):
+            b, j0 = divmod(load * LOAD_TILES, TILES_PER_BATCH)
+            x_sb = x_pool.tile([P, LOAD_TILES * HID], BF16)
+            nc.sync.dma_start(
+                out=x_sb[:], in_=x_view[b, :, j0 : j0 + LOAD_TILES, :].rearrange("p j k -> p (j k)")
+            )
+            return x_sb
+
+        x_tiles = [load_tokens(0)]
+        w_raw = const.tile([P, PACK, COLS], BF16)
+        nc.sync.dma_start(out=w_raw[:], in_=Wq.rearrange("(q t) c -> q t c", t=PACK))
+        cos_sb = const.tile([P, TILES_PER_BATCH, PAIRS], BF16)
+        nc.sync.dma_start(out=cos_sb[:], in_=rope_cos.rearrange("(p j) i -> p j i", p=P))
+        sin_sb = const.tile([P, TILES_PER_BATCH, PAIRS], BF16)
+        nc.sync.dma_start(out=sin_sb[:], in_=rope_sin.rearrange("(p j) i -> p j i", p=P))
+        for load in range(1, LOADS):
+            x_tiles.append(load_tokens(load))
+
+        ident = const.tile([P, P], F32)
+        make_identity(nc, ident[:])
+
+        w_grouped = const.tile([P, COLS, PACK], BF16, align_bytes=64)
+        nc.vector.tensor_copy(
+            out=w_grouped[:, 0:PLAIN_COLS, :].rearrange("q (h d) t -> q h d t", h=HEADS),
+            in_=w_raw[:].rearrange("q t (h z d) -> q z h d t", h=HEADS, z=2)[:, 0],
+        )
+        for e in range(2):
+            first = PLAIN_COLS + e * PLANE
+            nc.vector.tensor_copy(
+                out=w_grouped[:, first : first + PLANE, :].rearrange("q (h i) t -> q h i t", h=HEADS),
+                in_=w_raw[:].rearrange("q t (h z i e) -> q z e h i t", h=HEADS, z=2, e=2)[:, 1, e],
+            )
+        w_codes = const.tile([P, COLS], U32, align_bytes=64)
+        w_scales = const.tile([P, COLS], U8, align_bytes=64)
+        nc.vector.quantize_mx(
+            out=w_codes[:].bitcast(FP8X4),
+            scales=w_scales[:],
+            in_=w_grouped[:].rearrange("q c t -> q (c t)"),
+        )
+
+        even_factors = const.tile([P, TILES_PER_BATCH, PAIRS, 2], BF16)
+        odd_factors = const.tile([P, TILES_PER_BATCH, PAIRS, 2], BF16)
+        nc.vector.tensor_copy(out=even_factors[:, :, :, 0], in_=cos_sb[:])
+        nc.vector.tensor_copy(out=even_factors[:, :, :, 1], in_=sin_sb[:])
+        nc.vector.tensor_scalar_mul(out=odd_factors[:, :, :, 0], in0=sin_sb[:], scalar1=-1.0)
+        nc.vector.tensor_copy(out=odd_factors[:, :, :, 1], in_=cos_sb[:])
+
+        def transpose_and_quantise(step):
+            words = x_tiles[step // STEPS_PER_LOAD][:].bitcast(F32)
+            first_word = (step % STEPS_PER_LOAD) * STEP_TILES * WORDS
+            xt = xt_pool.tile([P, STEP_TILES, 2, P], F32)
+            for t in range(STEP_TILES):
+                for u in range(2):
+                    start = first_word + t * WORDS
+                    nc.tensor.transpose(xt[:, t, u, :], words[:, start + u : start + WORDS : 2], ident[:])
+            grouped = grouped_pool.tile([P, STEP_TILES * P * PACK], BF16, align_bytes=64)
+            nc.scalar.copy(
+                out=grouped[:].bitcast(F32).rearrange("q (t n u) -> q t n u", t=STEP_TILES, u=2),
+                in_=xt[:].rearrange("q t u n -> q t n u"),
+            )
+            x_codes = mx_pool.tile([P, STEP_TILES * P], U32, align_bytes=64)
+            x_scales = mx_pool.tile([P, STEP_TILES * P], U8, align_bytes=64)
+            nc.vector.quantize_mx(out=x_codes[:].bitcast(FP8X4), scales=x_scales[:], in_=grouped[:])
+            return x_codes, x_scales
+
+        def project_and_rotate(step, x_codes, x_scales):
+            b, step_in_batch = divmod(step, STEPS_PER_BATCH)
+            plain = plain_pool.tile([P, STEP_TILES, PLAIN_COLS], F32)
+            rope = rope_pool.tile([P, STEP_TILES, 2, PLANE], F32)
+            for t in range(STEP_TILES):
+                tokens = slice(t * P, (t + 1) * P)
+                nc.tensor.matmul_mx(
+                    out=plain[:, t, :],
+                    lhsT=x_codes[:, tokens].bitcast(FP8X4),
+                    lhsT_scale=x_scales[:, tokens],
+                    rhs=w_codes[:, 0:PLAIN_COLS].bitcast(FP8X4),
+                    rhs_scale=w_scales[:, 0:PLAIN_COLS],
+                    start=True,
+                    stop=True,
+                )
+                nc.tensor.matmul_mx(
+                    out=rope[:, t, :, :].rearrange("p e c -> p (e c)"),
+                    lhsT=x_codes[:, tokens].bitcast(FP8X4),
+                    lhsT_scale=x_scales[:, tokens],
+                    rhs=w_codes[:, PLAIN_COLS:COLS].bitcast(FP8X4),
+                    rhs_scale=w_scales[:, PLAIN_COLS:COLS],
+                    start=True,
+                    stop=True,
+                )
+
+            result = out_pool.tile([P, STEP_TILES, HEADS, HEAD_DIM], F32)
+            nc.scalar.copy(
+                out=result[:, :, :, 0:NOPE],
+                in_=plain[:].rearrange("p t (h d) -> p t h d", h=HEADS),
+            )
+
+            j0 = step_in_batch * STEP_TILES
+            shape = [P, STEP_TILES, HEADS, PAIRS, 2]
+            from_even = product_pool.tile(shape, F32)
+            from_odd = product_pool.tile(shape, F32)
+            for member, factors, product in ((0, even_factors, from_even), (1, odd_factors, from_odd)):
+                nc.vector.tensor_tensor(
+                    out=product[:],
+                    in0=rope[:, :, member, :]
+                    .rearrange("p t (h i) -> p t h i", h=HEADS)
+                    .unsqueeze(4)
+                    .to_broadcast(shape),
+                    in1=factors[:, j0 : j0 + STEP_TILES].unsqueeze(2).to_broadcast(shape),
+                    op=MULT,
+                )
+            nc.gpsimd.tensor_tensor(
+                out=result[:, :, :, NOPE:HEAD_DIM],
+                in0=from_even[:].rearrange("p t h i e -> p t h (i e)"),
+                in1=from_odd[:].rearrange("p t h i e -> p t h (i e)"),
+                op=ADD,
+            )
+            nc.sync.dma_start(
+                out=out_view[b, :, j0 : j0 + STEP_TILES, :],
+                in_=result[:].rearrange("p t h d -> p t (h d)"),
+            )
+
+        staged = transpose_and_quantise(0)
+        for step in range(STEPS):
+            following = transpose_and_quantise(step + 1) if step + 1 < STEPS else None
+            project_and_rotate(step, staged[0], staged[1])
+            staged = following

@@ -24,10 +24,10 @@ TILES_PER_BATCH = TOKENS // P
 STEP_TILES = 2
 STEPS_PER_BATCH = TILES_PER_BATCH // STEP_TILES
 STEPS = BATCH * STEPS_PER_BATCH
-LOAD_TILES = 4
-STEPS_PER_LOAD = LOAD_TILES // STEP_TILES
-LOADS = BATCH * TILES_PER_BATCH // LOAD_TILES
 WORDS = HID // 2
+GROUPS = (1, 1) + (2,) * ((STEPS - 2) // 2)
+AHEAD = 2
+LOAD_TILES = (2, 2, 4, 8, 16, 16, 16)
 
 FLOPS = 2 * BATCH * TOKENS * HID * COLS
 
@@ -39,104 +39,129 @@ def tile_multilatentattention_pb_t_kernel(tc, hidden_states, rope_cos, rope_sin,
 
     with ExitStack() as ctx:
         const = ctx.enter_context(tc.tile_pool(name="const", bufs=1))
-        x_pool = ctx.enter_context(tc.tile_pool(name="x", bufs=LOADS))
+        x_pool = ctx.enter_context(tc.tile_pool(name="x", bufs=1))
         grouped_pool = ctx.enter_context(tc.tile_pool(name="grouped", bufs=3))
-        mx_pool = ctx.enter_context(tc.tile_pool(name="mx", bufs=3))
-        product_pool = ctx.enter_context(tc.tile_pool(name="product", bufs=3))
-        out_pool = ctx.enter_context(tc.tile_pool(name="result", bufs=8))
+        mx_pool = ctx.enter_context(tc.tile_pool(name="mx", bufs=4))
+        product_pool = ctx.enter_context(tc.tile_pool(name="product", bufs=4))
+        out_pool = ctx.enter_context(tc.tile_pool(name="result", bufs=12))
         xt_pool = ctx.enter_context(tc.psum_pool(name="xt", bufs=2))
-        plain_pool = ctx.enter_context(tc.psum_pool(name="plain", bufs=3))
-        rope_pool = ctx.enter_context(tc.psum_pool(name="rope", bufs=3))
-
-        def load_tokens(load):
-            b, j0 = divmod(load * LOAD_TILES, TILES_PER_BATCH)
-            x_sb = x_pool.tile([P, LOAD_TILES * HID], BF16)
-            nc.sync.dma_start(
-                out=x_sb[:], in_=x_view[b, :, j0 : j0 + LOAD_TILES, :].rearrange("p j k -> p (j k)")
-            )
-            return x_sb
-
-        x_tiles = [load_tokens(0)]
-        w_raw = const.tile([P, PACK, COLS], BF16)
-        nc.sync.dma_start(out=w_raw[:], in_=Wq.rearrange("(q t) c -> q t c", t=PACK))
-        cos_sb = const.tile([P, TILES_PER_BATCH, PAIRS], BF16)
-        nc.sync.dma_start(out=cos_sb[:], in_=rope_cos.rearrange("(p j) i -> p j i", p=P))
-        sin_sb = const.tile([P, TILES_PER_BATCH, PAIRS], BF16)
-        nc.sync.dma_start(out=sin_sb[:], in_=rope_sin.rearrange("(p j) i -> p j i", p=P))
-        for load in range(1, LOADS):
-            x_tiles.append(load_tokens(load))
+        plain_pool = ctx.enter_context(tc.psum_pool(name="plain", bufs=2))
+        rope_pool = ctx.enter_context(tc.psum_pool(name="rope", bufs=4))
+        ctx.enter_context(tc.manual_schedule())
 
         ident = const.tile([P, P], F32)
         make_identity(nc, ident[:])
 
+        w_raw = const.tile([P, PACK, COLS], BF16)
+        nc.sync.dma_start(out=w_raw[:], in_=Wq.rearrange("(q t) c -> q t c", t=PACK))
+
+        step_words = []
+
+        def load_tokens(load):
+            first, count = sum(LOAD_TILES[:load]), LOAD_TILES[load]
+            b, j0 = divmod(first, TILES_PER_BATCH)
+            x_sb = x_pool.tile([P, count * HID], BF16, name="x_sb_%d" % load)
+            nc.sync.dma_start(
+                out=x_sb[:], in_=x_view[b, :, j0 : j0 + count, :].rearrange("p j k -> p (j k)")
+            )
+            for j in range(0, count, STEP_TILES):
+                step_words.append((x_sb[:].bitcast(F32), j * WORDS))
+
+        load_tokens(0)
+        cos_sb = const.tile([P, TILES_PER_BATCH, PAIRS], BF16)
+        nc.sync.dma_start(out=cos_sb[:], in_=rope_cos.rearrange("(p j) i -> p j i", p=P))
+        sin_sb = const.tile([P, TILES_PER_BATCH, PAIRS], BF16)
+        nc.sync.dma_start(out=sin_sb[:], in_=rope_sin.rearrange("(p j) i -> p j i", p=P))
+        for load in range(1, len(LOAD_TILES)):
+            load_tokens(load)
+
+        ROTATED = 2 * PLANE
         w_grouped = const.tile([P, COLS, PACK], BF16, align_bytes=64)
-        nc.vector.tensor_copy(
-            out=w_grouped[:, 0:PLAIN_COLS, :].rearrange("q (h d) t -> q h d t", h=HEADS),
-            in_=w_raw[:].rearrange("q t (h z d) -> q z h d t", h=HEADS, z=2)[:, 0],
-        )
         for e in range(2):
-            first = PLAIN_COLS + e * PLANE
             nc.vector.tensor_copy(
-                out=w_grouped[:, first : first + PLANE, :].rearrange("q (h i) t -> q h i t", h=HEADS),
+                out=w_grouped[:, e * PLANE : (e + 1) * PLANE, :].rearrange("q (h i) t -> q h i t", h=HEADS),
                 in_=w_raw[:].rearrange("q t (h z i e) -> q z e h i t", h=HEADS, z=2, e=2)[:, 1, e],
             )
+        nc.scalar.copy(
+            out=w_grouped[:, ROTATED:COLS, :].rearrange("q (h d) t -> q h d t", h=HEADS),
+            in_=w_raw[:].rearrange("q t (h z d) -> q z h d t", h=HEADS, z=2)[:, 0],
+        )
         w_codes = const.tile([P, COLS], U32, align_bytes=64)
         w_scales = const.tile([P, COLS], U8, align_bytes=64)
-        nc.vector.quantize_mx(
-            out=w_codes[:].bitcast(FP8X4),
-            scales=w_scales[:],
-            in_=w_grouped[:].rearrange("q c t -> q (c t)"),
-        )
+
+        def quantise_w(cols):
+            nc.vector.quantize_mx(
+                out=w_codes[:, cols].bitcast(FP8X4),
+                scales=w_scales[:, cols],
+                in_=w_grouped[:, cols, :].rearrange("q c t -> q (c t)"),
+            )
 
         even_factors = const.tile([P, TILES_PER_BATCH, PAIRS, 2], BF16)
         odd_factors = const.tile([P, TILES_PER_BATCH, PAIRS, 2], BF16)
-        nc.vector.tensor_copy(out=even_factors[:, :, :, 0], in_=cos_sb[:])
-        nc.vector.tensor_copy(out=even_factors[:, :, :, 1], in_=sin_sb[:])
-        nc.vector.tensor_scalar_mul(out=odd_factors[:, :, :, 0], in0=sin_sb[:], scalar1=-1.0)
-        nc.vector.tensor_copy(out=odd_factors[:, :, :, 1], in_=cos_sb[:])
+        for tiles in (slice(0, LOAD_TILES[0]), slice(LOAD_TILES[0], TILES_PER_BATCH)):
+            for factors, e, source, sign in (
+                (even_factors, 0, cos_sb, 1.0),
+                (even_factors, 1, sin_sb, 1.0),
+                (odd_factors, 0, sin_sb, -1.0),
+                (odd_factors, 1, cos_sb, 1.0),
+            ):
+                nc.gpsimd.tensor_scalar(
+                    out=factors[:, tiles, :, e],
+                    in0=source[:, tiles, :],
+                    scalar1=sign,
+                    scalar2=0.0,
+                    op0=MULT,
+                    op1=ADD,
+                )
 
-        def transpose_and_quantise(step):
-            words = x_tiles[step // STEPS_PER_LOAD][:].bitcast(F32)
-            first_word = (step % STEPS_PER_LOAD) * STEP_TILES * WORDS
-            xt = xt_pool.tile([P, STEP_TILES, 2, P], F32)
-            for t in range(STEP_TILES):
-                for u in range(2):
+        def transpose(first_step, steps):
+            grouped = grouped_pool.tile([P, 2 * STEP_TILES * P * PACK], BF16, align_bytes=64)
+            half = STEP_TILES * P * PACK
+            for s in range(steps):
+                words, first_word = step_words[first_step + s]
+                xt = xt_pool.tile([P, STEP_TILES, 2, P], F32)
+                for t in range(STEP_TILES):
                     start = first_word + t * WORDS
-                    nc.tensor.transpose(xt[:, t, u, :], words[:, start + u : start + WORDS : 2], ident[:])
-            grouped = grouped_pool.tile([P, STEP_TILES * P * PACK], BF16, align_bytes=64)
-            nc.scalar.copy(
-                out=grouped[:].bitcast(F32).rearrange("q (t n u) -> q t n u", t=STEP_TILES, u=2),
-                in_=xt[:].rearrange("q t u n -> q t n u"),
+                    for u in range(2):
+                        nc.tensor.transpose(xt[:, t, u, :], words[:, start + u : start + WORDS : 2], ident[:])
+                nc.scalar.copy(
+                    out=grouped[:, s * half : (s + 1) * half]
+                    .bitcast(F32)
+                    .rearrange("q (t n u) -> q t n u", t=STEP_TILES, u=2),
+                    in_=xt[:].rearrange("q t u n -> q t n u"),
+                )
+            return grouped
+
+        def quantise(grouped, steps):
+            tokens = steps * STEP_TILES * P
+            x_codes = mx_pool.tile([P, 2 * STEP_TILES * P], U32, align_bytes=64)
+            x_scales = mx_pool.tile([P, 2 * STEP_TILES * P], U8, align_bytes=64)
+            nc.vector.quantize_mx(
+                out=x_codes[:, 0:tokens].bitcast(FP8X4),
+                scales=x_scales[:, 0:tokens],
+                in_=grouped[:, 0 : tokens * PACK],
             )
-            x_codes = mx_pool.tile([P, STEP_TILES * P], U32, align_bytes=64)
-            x_scales = mx_pool.tile([P, STEP_TILES * P], U8, align_bytes=64)
-            nc.vector.quantize_mx(out=x_codes[:].bitcast(FP8X4), scales=x_scales[:], in_=grouped[:])
             return x_codes, x_scales
 
-        def project_and_rotate(step, x_codes, x_scales):
+        def project_and_rotate(step, x_codes, x_scales, first_token):
             b, step_in_batch = divmod(step, STEPS_PER_BATCH)
-            plain = plain_pool.tile([P, STEP_TILES, PLAIN_COLS], F32)
             rope = rope_pool.tile([P, STEP_TILES, 2, PLANE], F32)
-            for t in range(STEP_TILES):
-                tokens = slice(t * P, (t + 1) * P)
-                nc.tensor.matmul_mx(
-                    out=plain[:, t, :],
-                    lhsT=x_codes[:, tokens].bitcast(FP8X4),
-                    lhsT_scale=x_scales[:, tokens],
-                    rhs=w_codes[:, 0:PLAIN_COLS].bitcast(FP8X4),
-                    rhs_scale=w_scales[:, 0:PLAIN_COLS],
-                    start=True,
-                    stop=True,
-                )
-                nc.tensor.matmul_mx(
-                    out=rope[:, t, :, :].rearrange("p e c -> p (e c)"),
-                    lhsT=x_codes[:, tokens].bitcast(FP8X4),
-                    lhsT_scale=x_scales[:, tokens],
-                    rhs=w_codes[:, PLAIN_COLS:COLS].bitcast(FP8X4),
-                    rhs_scale=w_scales[:, PLAIN_COLS:COLS],
-                    start=True,
-                    stop=True,
-                )
+            plain = plain_pool.tile([P, STEP_TILES, PLAIN_COLS], F32)
+            for bank, cols in (
+                (rope[:].rearrange("p t e c -> p t (e c)"), slice(0, ROTATED)),
+                (plain[:], slice(ROTATED, COLS)),
+            ):
+                for t in range(STEP_TILES):
+                    tokens = slice(first_token + t * P, first_token + (t + 1) * P)
+                    nc.tensor.matmul_mx(
+                        out=bank[:, t, :],
+                        lhsT=x_codes[:, tokens].bitcast(FP8X4),
+                        lhsT_scale=x_scales[:, tokens],
+                        rhs=w_codes[:, cols].bitcast(FP8X4),
+                        rhs_scale=w_scales[:, cols],
+                        start=True,
+                        stop=True,
+                    )
 
             result = out_pool.tile([P, STEP_TILES, HEADS, HEAD_DIM], F32)
             nc.scalar.copy(
@@ -158,7 +183,8 @@ def tile_multilatentattention_pb_t_kernel(tc, hidden_states, rope_cos, rope_sin,
                     in1=factors[:, j0 : j0 + STEP_TILES].unsqueeze(2).to_broadcast(shape),
                     op=MULT,
                 )
-            nc.gpsimd.tensor_tensor(
+            adder = nc.vector if step == STEPS - 1 else nc.gpsimd
+            adder.tensor_tensor(
                 out=result[:, :, :, NOPE:HEAD_DIM],
                 in0=from_even[:].rearrange("p t h i e -> p t h (i e)"),
                 in1=from_odd[:].rearrange("p t h i e -> p t h (i e)"),
@@ -169,8 +195,19 @@ def tile_multilatentattention_pb_t_kernel(tc, hidden_states, rope_cos, rope_sin,
                 in_=result[:].rearrange("p t h d -> p t (h d)"),
             )
 
-        staged = transpose_and_quantise(0)
-        for step in range(STEPS):
-            following = transpose_and_quantise(step + 1) if step + 1 < STEPS else None
-            project_and_rotate(step, staged[0], staged[1])
-            staged = following
+        firsts = [sum(GROUPS[:g]) for g in range(len(GROUPS))]
+        quantise_w(slice(0, ROTATED))
+        staged = []
+        for g in range(AHEAD):
+            grouped = transpose(firsts[g], GROUPS[g])
+            staged.append(quantise(grouped, GROUPS[g]))
+            if g == 0:
+                quantise_w(slice(ROTATED, COLS))
+        for g in range(len(GROUPS)):
+            ahead = g + AHEAD
+            if ahead < len(GROUPS):
+                grouped = transpose(firsts[ahead], GROUPS[ahead])
+            for s in range(GROUPS[g]):
+                project_and_rotate(firsts[g] + s, staged[g][0], staged[g][1], s * STEP_TILES * P)
+            if ahead < len(GROUPS):
+                staged.append(quantise(grouped, GROUPS[ahead]))

@@ -26,6 +26,7 @@ STEPS_PER_BATCH = TILES_PER_BATCH // STEP_TILES
 STEPS = BATCH * STEPS_PER_BATCH
 WORDS = HID // 2
 GROUPS = (1, 1) + (2,) * ((STEPS - 2) // 2)
+VECTOR_TILES = 1
 AHEAD = 2
 LOAD_TILES = (2, 2, 4, 8, 16, 16, 16)
 
@@ -42,8 +43,8 @@ def tile_multilatentattention_pb_t_kernel(tc, hidden_states, rope_cos, rope_sin,
         x_pool = ctx.enter_context(tc.tile_pool(name="x", bufs=1))
         grouped_pool = ctx.enter_context(tc.tile_pool(name="grouped", bufs=3))
         mx_pool = ctx.enter_context(tc.tile_pool(name="mx", bufs=4))
-        product_pool = ctx.enter_context(tc.tile_pool(name="product", bufs=4))
-        out_pool = ctx.enter_context(tc.tile_pool(name="result", bufs=12))
+        product_pool = ctx.enter_context(tc.tile_pool(name="product", bufs=3))
+        out_pool = ctx.enter_context(tc.tile_pool(name="result", bufs=6))
         xt_pool = ctx.enter_context(tc.psum_pool(name="xt", bufs=2))
         plain_pool = ctx.enter_context(tc.psum_pool(name="plain", bufs=2))
         rope_pool = ctx.enter_context(tc.psum_pool(name="rope", bufs=4))
@@ -143,8 +144,7 @@ def tile_multilatentattention_pb_t_kernel(tc, hidden_states, rope_cos, rope_sin,
             )
             return x_codes, x_scales
 
-        def project_and_rotate(step, x_codes, x_scales, first_token):
-            b, step_in_batch = divmod(step, STEPS_PER_BATCH)
+        def project(x_codes, x_scales, first_token):
             rope = rope_pool.tile([P, STEP_TILES, 2, PLANE], F32)
             plain = plain_pool.tile([P, STEP_TILES, PLAIN_COLS], F32)
             for bank, cols in (
@@ -162,37 +162,34 @@ def tile_multilatentattention_pb_t_kernel(tc, hidden_states, rope_cos, rope_sin,
                         start=True,
                         stop=True,
                     )
+            return rope, plain
 
-            result = out_pool.tile([P, STEP_TILES, HEADS, HEAD_DIM], F32)
-            nc.scalar.copy(
-                out=result[:, :, :, 0:NOPE],
-                in_=plain[:].rearrange("p t (h d) -> p t h d", h=HEADS),
+        def rotate(rope, member, j0, heads, product):
+            factors = odd_factors if member else even_factors
+            shape = [P, STEP_TILES, heads.stop - heads.start, PAIRS, 2]
+            nc.vector.tensor_tensor(
+                out=product[:, :, heads],
+                in0=rope[:, :, member, :]
+                .rearrange("p t (h i) -> p t h i", h=HEADS)[:, :, heads]
+                .unsqueeze(4)
+                .to_broadcast(shape),
+                in1=factors[:, j0 : j0 + STEP_TILES].unsqueeze(2).to_broadcast(shape),
+                op=MULT,
             )
 
-            j0 = step_in_batch * STEP_TILES
-            shape = [P, STEP_TILES, HEADS, PAIRS, 2]
-            from_even = product_pool.tile(shape, F32)
-            from_odd = product_pool.tile(shape, F32)
-            for member, factors, product in ((0, even_factors, from_even), (1, odd_factors, from_odd)):
-                nc.vector.tensor_tensor(
-                    out=product[:],
-                    in0=rope[:, :, member, :]
-                    .rearrange("p t (h i) -> p t h i", h=HEADS)
-                    .unsqueeze(4)
-                    .to_broadcast(shape),
-                    in1=factors[:, j0 : j0 + STEP_TILES].unsqueeze(2).to_broadcast(shape),
-                    op=MULT,
-                )
-            adder = nc.vector if step == STEPS - 1 else nc.gpsimd
-            adder.tensor_tensor(
-                out=result[:, :, :, NOPE:HEAD_DIM],
-                in0=from_even[:].rearrange("p t h i e -> p t h (i e)"),
-                in1=from_odd[:].rearrange("p t h i e -> p t h (i e)"),
+        def add(engine, tiles, from_even, from_odd, result):
+            engine.tensor_tensor(
+                out=result[:, tiles, :, NOPE:HEAD_DIM],
+                in0=from_even[:, tiles].rearrange("p t h i e -> p t h (i e)"),
+                in1=from_odd[:, tiles].rearrange("p t h i e -> p t h (i e)"),
                 op=ADD,
             )
+
+        def store(first_tile, tiles, result):
+            b, j = divmod(first_tile + tiles.start, TILES_PER_BATCH)
             nc.sync.dma_start(
-                out=out_view[b, :, j0 : j0 + STEP_TILES, :],
-                in_=result[:].rearrange("p t h d -> p t (h d)"),
+                out=out_view[b, :, j : j + tiles.stop - tiles.start, :],
+                in_=result[:, tiles].rearrange("p t h d -> p t (h d)"),
             )
 
         firsts = [sum(GROUPS[:g]) for g in range(len(GROUPS))]
@@ -203,11 +200,37 @@ def tile_multilatentattention_pb_t_kernel(tc, hidden_states, rope_cos, rope_sin,
             staged.append(quantise(grouped, GROUPS[g]))
             if g == 0:
                 quantise_w(slice(ROTATED, COLS))
+        all_heads, last_head = slice(0, HEADS), slice(HEADS - 1, HEADS)
         for g in range(len(GROUPS)):
             ahead = g + AHEAD
+            final = g == len(GROUPS) - 1
             if ahead < len(GROUPS):
                 grouped = transpose(firsts[ahead], GROUPS[ahead])
+            first_tile = firsts[g] * STEP_TILES
+            group_tiles = GROUPS[g] * STEP_TILES
+            group_shape = [P, 2 * STEP_TILES, HEADS]
+            result = out_pool.tile(group_shape + [HEAD_DIM], F32)
+            from_even = product_pool.tile(group_shape + [PAIRS, 2], F32)
+            from_odd = product_pool.tile(group_shape + [PAIRS, 2], F32)
             for s in range(GROUPS[g]):
-                project_and_rotate(firsts[g] + s, staged[g][0], staged[g][1], s * STEP_TILES * P)
-            if ahead < len(GROUPS):
-                staged.append(quantise(grouped, GROUPS[ahead]))
+                tiles = slice(s * STEP_TILES, (s + 1) * STEP_TILES)
+                j0 = (first_tile + tiles.start) % TILES_PER_BATCH
+                rope, plain = project(staged[g][0], staged[g][1], tiles.start * P)
+                nc.scalar.copy(
+                    out=result[:, tiles, :, 0:NOPE],
+                    in_=plain[:].rearrange("p t (h d) -> p t h d", h=HEADS),
+                )
+                split = s == 1 and not final
+                rotate(rope, 0, j0, all_heads, from_even[:, tiles])
+                rotate(rope, 1, j0, slice(0, HEADS - 1) if split else all_heads, from_odd[:, tiles])
+                if final:
+                    add(nc.vector, tiles, from_even, from_odd, result)
+                    store(first_tile, tiles, result)
+            if not final:
+                add(nc.vector, slice(0, VECTOR_TILES), from_even, from_odd, result)
+                if ahead < len(GROUPS):
+                    staged.append(quantise(grouped, GROUPS[ahead]))
+                if split:
+                    rotate(rope, 1, j0, last_head, from_odd[:, tiles])
+                add(nc.gpsimd, slice(VECTOR_TILES, group_tiles), from_even, from_odd, result)
+                store(first_tile, slice(0, group_tiles), result)

@@ -10,6 +10,7 @@ U8 = mybir.dt.uint8
 FP8X4 = mybir.dt.float8_e4m3fn_x4
 MULT = mybir.AluOpType.mult
 ADD = mybir.AluOpType.add
+SUBTRACT = mybir.AluOpType.subtract
 
 P = 128
 PACK = 4
@@ -26,7 +27,6 @@ STEPS_PER_BATCH = TILES_PER_BATCH // STEP_TILES
 STEPS = BATCH * STEPS_PER_BATCH
 WORDS = HID // 2
 GROUPS = (1, 1) + (2,) * ((STEPS - 2) // 2)
-VECTOR_TILES = 1
 AHEAD = 2
 LOAD_TILES = (2, 2, 4, 8, 16, 16, 16)
 
@@ -47,7 +47,8 @@ def tile_multilatentattention_pb_t_kernel(tc, hidden_states, rope_cos, rope_sin,
         out_pool = ctx.enter_context(tc.tile_pool(name="result", bufs=6))
         xt_pool = ctx.enter_context(tc.psum_pool(name="xt", bufs=2))
         plain_pool = ctx.enter_context(tc.psum_pool(name="plain", bufs=2))
-        rope_pool = ctx.enter_context(tc.psum_pool(name="rope", bufs=4))
+        members_pool = ctx.enter_context(tc.psum_pool(name="members", bufs=2))
+        sums_pool = ctx.enter_context(tc.psum_pool(name="sums", bufs=2))
         ctx.enter_context(tc.manual_schedule())
 
         ident = const.tile([P, P], F32)
@@ -81,7 +82,7 @@ def tile_multilatentattention_pb_t_kernel(tc, hidden_states, rope_cos, rope_sin,
         for e in range(2):
             nc.vector.tensor_copy(
                 out=w_grouped[:, e * PLANE : (e + 1) * PLANE, :].rearrange("q (h i) t -> q h i t", h=HEADS),
-                in_=w_raw[:].rearrange("q t (h z i e) -> q z e h i t", h=HEADS, z=2, e=2)[:, 1, e],
+                in_=w_raw[:].rearrange("q t (h z i e) -> q z e h i t", h=HEADS, z=2, e=2)[:, 1, 1 - e],
             )
         nc.scalar.copy(
             out=w_grouped[:, ROTATED:COLS, :].rearrange("q (h d) t -> q h d t", h=HEADS),
@@ -97,22 +98,15 @@ def tile_multilatentattention_pb_t_kernel(tc, hidden_states, rope_cos, rope_sin,
                 in_=w_grouped[:, cols, :].rearrange("q c t -> q (c t)"),
             )
 
-        even_factors = const.tile([P, TILES_PER_BATCH, PAIRS, 2], BF16)
-        odd_factors = const.tile([P, TILES_PER_BATCH, PAIRS, 2], BF16)
+        minus_cos = const.tile([P, TILES_PER_BATCH, PAIRS], BF16)
+        member_factors = const.tile([P, TILES_PER_BATCH, PAIRS, 2], F32)
         for tiles in (slice(0, LOAD_TILES[0]), slice(LOAD_TILES[0], TILES_PER_BATCH)):
-            for factors, e, source, sign in (
-                (even_factors, 0, cos_sb, 1.0),
-                (even_factors, 1, sin_sb, 1.0),
-                (odd_factors, 0, sin_sb, -1.0),
-                (odd_factors, 1, cos_sb, 1.0),
-            ):
-                nc.gpsimd.tensor_scalar(
-                    out=factors[:, tiles, :, e],
-                    in0=source[:, tiles, :],
-                    scalar1=sign,
-                    scalar2=0.0,
-                    op0=MULT,
-                    op1=ADD,
+            nc.gpsimd.tensor_scalar(
+                out=minus_cos[:, tiles], in0=cos_sb[:, tiles], scalar1=-1.0, scalar2=0.0, op0=MULT, op1=ADD
+            )
+            for e, op in ((0, SUBTRACT), (1, ADD)):
+                nc.gpsimd.tensor_tensor(
+                    out=member_factors[:, tiles, :, e], in0=minus_cos[:, tiles], in1=sin_sb[:, tiles], op=op
                 )
 
         def transpose(first_step, steps):
@@ -144,44 +138,47 @@ def tile_multilatentattention_pb_t_kernel(tc, hidden_states, rope_cos, rope_sin,
             )
             return x_codes, x_scales
 
-        def project(x_codes, x_scales, first_token):
-            rope = rope_pool.tile([P, STEP_TILES, 2, PLANE], F32)
-            plain = plain_pool.tile([P, STEP_TILES, PLAIN_COLS], F32)
-            for bank, cols in (
-                (rope[:].rearrange("p t e c -> p t (e c)"), slice(0, ROTATED)),
-                (plain[:], slice(ROTATED, COLS)),
-            ):
-                for t in range(STEP_TILES):
-                    tokens = slice(first_token + t * P, first_token + (t + 1) * P)
-                    nc.tensor.matmul_mx(
-                        out=bank[:, t, :],
-                        lhsT=x_codes[:, tokens].bitcast(FP8X4),
-                        lhsT_scale=x_scales[:, tokens],
-                        rhs=w_codes[:, cols].bitcast(FP8X4),
-                        rhs_scale=w_scales[:, cols],
-                        start=True,
-                        stop=True,
-                    )
-            return rope, plain
+        def multiply(bank, x_codes, x_scales, tile, cols, start=True, stop=True):
+            tokens = slice(tile * P, (tile + 1) * P)
+            nc.tensor.matmul_mx(
+                out=bank,
+                lhsT=x_codes[:, tokens].bitcast(FP8X4),
+                lhsT_scale=x_scales[:, tokens],
+                rhs=w_codes[:, cols].bitcast(FP8X4),
+                rhs_scale=w_scales[:, cols],
+                start=start,
+                stop=stop,
+            )
 
-        def rotate(rope, member, j0, heads, product):
-            factors = odd_factors if member else even_factors
-            shape = [P, STEP_TILES, heads.stop - heads.start, PAIRS, 2]
+        def scale_sums(tiles, first_tile, sums, scaled_sums):
+            j0, count = (first_tile + tiles.start) % TILES_PER_BATCH, tiles.stop - tiles.start
+            shape = [P, count, HEADS, PAIRS]
             nc.vector.tensor_tensor(
-                out=product[:, :, heads],
-                in0=rope[:, :, member, :]
-                .rearrange("p t (h i) -> p t h i", h=HEADS)[:, :, heads]
-                .unsqueeze(4)
-                .to_broadcast(shape),
-                in1=factors[:, j0 : j0 + STEP_TILES].unsqueeze(2).to_broadcast(shape),
+                out=scaled_sums[:, tiles].rearrange("p t (h i) -> p t h i", h=HEADS),
+                in0=sums[:, tiles].rearrange("p t (h i) -> p t h i", h=HEADS),
+                in1=cos_sb[:, j0 : j0 + count].unsqueeze(2).to_broadcast(shape),
                 op=MULT,
             )
 
-        def add(engine, tiles, from_even, from_odd, result):
+        def scale_members(tiles, first_tile, members, scaled_members):
+            j0, count = (first_tile + tiles.start) % TILES_PER_BATCH, tiles.stop - tiles.start
+            shape = [P, count, HEADS, PAIRS, 2]
+            nc.vector.tensor_tensor(
+                out=scaled_members[:, tiles].rearrange("p t (h i) e -> p t h i e", h=HEADS),
+                in0=members[:].rearrange("p t e (h i) -> p t h i e", h=HEADS),
+                in1=member_factors[:, j0 : j0 + count].unsqueeze(2).to_broadcast(shape),
+                op=MULT,
+            )
+
+        def add(engine, tiles, scaled_sums, scaled_members, result):
+            shape = [P, tiles.stop - tiles.start, HEADS, PAIRS, 2]
             engine.tensor_tensor(
-                out=result[:, tiles, :, NOPE:HEAD_DIM],
-                in0=from_even[:, tiles].rearrange("p t h i e -> p t h (i e)"),
-                in1=from_odd[:, tiles].rearrange("p t h i e -> p t h (i e)"),
+                out=result[:, tiles, :, NOPE:HEAD_DIM].rearrange("p t h (i e) -> p t h i e", e=2),
+                in0=scaled_sums[:, tiles]
+                .rearrange("p t (h i) -> p t h i", h=HEADS)
+                .unsqueeze(4)
+                .to_broadcast(shape),
+                in1=scaled_members[:, tiles].rearrange("p t (h i) e -> p t h i e", h=HEADS),
                 op=ADD,
             )
 
@@ -200,37 +197,50 @@ def tile_multilatentattention_pb_t_kernel(tc, hidden_states, rope_cos, rope_sin,
             staged.append(quantise(grouped, GROUPS[g]))
             if g == 0:
                 quantise_w(slice(ROTATED, COLS))
-        all_heads, last_head = slice(0, HEADS), slice(HEADS - 1, HEADS)
+        first_half, second_half = slice(0, STEP_TILES), slice(STEP_TILES, 2 * STEP_TILES)
         for g in range(len(GROUPS)):
             ahead = g + AHEAD
             final = g == len(GROUPS) - 1
             if ahead < len(GROUPS):
                 grouped = transpose(firsts[ahead], GROUPS[ahead])
             first_tile = firsts[g] * STEP_TILES
-            group_tiles = GROUPS[g] * STEP_TILES
-            group_shape = [P, 2 * STEP_TILES, HEADS]
-            result = out_pool.tile(group_shape + [HEAD_DIM], F32)
-            from_even = product_pool.tile(group_shape + [PAIRS, 2], F32)
-            from_odd = product_pool.tile(group_shape + [PAIRS, 2], F32)
-            for s in range(GROUPS[g]):
-                tiles = slice(s * STEP_TILES, (s + 1) * STEP_TILES)
-                j0 = (first_tile + tiles.start) % TILES_PER_BATCH
-                rope, plain = project(staged[g][0], staged[g][1], tiles.start * P)
+            halves = (first_half, second_half)[: GROUPS[g]]
+            x_codes, x_scales = staged[g]
+
+            sums = sums_pool.tile([P, 2 * STEP_TILES, PLANE], F32)
+            for tile in range(GROUPS[g] * STEP_TILES):
+                multiply(sums[:, tile], x_codes, x_scales, tile, slice(0, PLANE), stop=False)
+                multiply(sums[:, tile], x_codes, x_scales, tile, slice(PLANE, ROTATED), start=False)
+            members = []
+            for half in halves:
+                bank = members_pool.tile([P, STEP_TILES, 2, PLANE], F32)
+                for t in range(STEP_TILES):
+                    out_cols = bank[:, t].rearrange("p e c -> p (e c)")
+                    multiply(out_cols, x_codes, x_scales, half.start + t, slice(0, ROTATED))
+                members.append(bank)
+            result = out_pool.tile([P, 2 * STEP_TILES, HEADS, HEAD_DIM], F32)
+            for half in halves:
+                plain = plain_pool.tile([P, STEP_TILES, PLAIN_COLS], F32)
+                for t in range(STEP_TILES):
+                    multiply(plain[:, t], x_codes, x_scales, half.start + t, slice(ROTATED, COLS))
                 nc.scalar.copy(
-                    out=result[:, tiles, :, 0:NOPE],
+                    out=result[:, half, :, 0:NOPE],
                     in_=plain[:].rearrange("p t (h d) -> p t h d", h=HEADS),
                 )
-                split = s == 1 and not final
-                rotate(rope, 0, j0, all_heads, from_even[:, tiles])
-                rotate(rope, 1, j0, slice(0, HEADS - 1) if split else all_heads, from_odd[:, tiles])
-                if final:
-                    add(nc.vector, tiles, from_even, from_odd, result)
-                    store(first_tile, tiles, result)
-            if not final:
-                add(nc.vector, slice(0, VECTOR_TILES), from_even, from_odd, result)
-                if ahead < len(GROUPS):
-                    staged.append(quantise(grouped, GROUPS[ahead]))
-                if split:
-                    rotate(rope, 1, j0, last_head, from_odd[:, tiles])
-                add(nc.gpsimd, slice(VECTOR_TILES, group_tiles), from_even, from_odd, result)
-                store(first_tile, slice(0, group_tiles), result)
+
+            scaled_sums = product_pool.tile([P, 2 * STEP_TILES, PLANE], F32)
+            scaled_members = product_pool.tile([P, 2 * STEP_TILES, PLANE, 2], F32)
+            scale_sums(first_half, first_tile, sums, scaled_sums)
+            for half, bank in zip(halves, members):
+                scale_members(half, first_tile, bank, scaled_members)
+            add(nc.vector, first_half, scaled_sums, scaled_members, result)
+            if ahead < len(GROUPS):
+                staged.append(quantise(grouped, GROUPS[ahead]))
+            if GROUPS[g] > 1:
+                scale_sums(second_half, first_tile, sums, scaled_sums)
+                add(nc.vector if final else nc.gpsimd, second_half, scaled_sums, scaled_members, result)
+            if final:
+                for half in halves:
+                    store(first_tile, half, result)
+            else:
+                store(first_tile, slice(0, GROUPS[g] * STEP_TILES), result)

from contextlib import ExitStack

import concourse.mybir as mybir
from concourse.masks import make_identity

F32 = mybir.dt.float32
BF16 = mybir.dt.bfloat16
U32 = mybir.dt.uint32
U8 = mybir.dt.uint8
FP8X4 = mybir.dt.float8_e4m3fn_x4
MULT = mybir.AluOpType.mult
ADD = mybir.AluOpType.add
SUBTRACT = mybir.AluOpType.subtract

P = 128
PACK = 4
BATCH, TOKENS, HID = 4, 2048, 512
HEADS, HEAD_DIM = 4, 128
NOPE = 64
PAIRS = 32
COLS = HEADS * HEAD_DIM
PLAIN_COLS = HEADS * NOPE
PLANE = HEADS * PAIRS
TILES_PER_BATCH = TOKENS // P
STEP_TILES = 2
STEPS_PER_BATCH = TILES_PER_BATCH // STEP_TILES
STEPS = BATCH * STEPS_PER_BATCH
WORDS = HID // 2
GROUPS = (1, 1) + (2,) * ((STEPS - 2) // 2)
AHEAD = 2
LOAD_TILES = (2, 2, 4, 8, 16, 16, 16)

FLOPS = 2 * BATCH * TOKENS * HID * COLS


def tile_multilatentattention_pb_t_kernel(tc, hidden_states, rope_cos, rope_sin, Wq, out):
    nc = tc.nc
    x_view = hidden_states.rearrange("b (p j) k -> b p j k", p=P)
    out_view = out.rearrange("b (p j) h d -> b p j (h d)", p=P)

    with ExitStack() as ctx:
        const = ctx.enter_context(tc.tile_pool(name="const", bufs=1))
        x_pool = ctx.enter_context(tc.tile_pool(name="x", bufs=1))
        grouped_pool = ctx.enter_context(tc.tile_pool(name="grouped", bufs=3))
        mx_pool = ctx.enter_context(tc.tile_pool(name="mx", bufs=4))
        product_pool = ctx.enter_context(tc.tile_pool(name="product", bufs=3))
        out_pool = ctx.enter_context(tc.tile_pool(name="result", bufs=6))
        xt_pool = ctx.enter_context(tc.psum_pool(name="xt", bufs=2))
        plain_pool = ctx.enter_context(tc.psum_pool(name="plain", bufs=2))
        members_pool = ctx.enter_context(tc.psum_pool(name="members", bufs=2))
        sums_pool = ctx.enter_context(tc.psum_pool(name="sums", bufs=2))
        ctx.enter_context(tc.manual_schedule())

        ident = const.tile([P, P], F32)
        make_identity(nc, ident[:])

        w_raw = const.tile([P, PACK, COLS], BF16)
        nc.sync.dma_start(out=w_raw[:], in_=Wq.rearrange("(q t) c -> q t c", t=PACK))

        step_words = []

        def load_tokens(load):
            first, count = sum(LOAD_TILES[:load]), LOAD_TILES[load]
            b, j0 = divmod(first, TILES_PER_BATCH)
            x_sb = x_pool.tile([P, count * HID], BF16, name="x_sb_%d" % load)
            nc.sync.dma_start(
                out=x_sb[:], in_=x_view[b, :, j0 : j0 + count, :].rearrange("p j k -> p (j k)")
            )
            for j in range(0, count, STEP_TILES):
                step_words.append((x_sb[:].bitcast(F32), j * WORDS))

        load_tokens(0)
        cos_sb = const.tile([P, TILES_PER_BATCH, PAIRS], BF16)
        nc.sync.dma_start(out=cos_sb[:], in_=rope_cos.rearrange("(p j) i -> p j i", p=P))
        sin_sb = const.tile([P, TILES_PER_BATCH, PAIRS], BF16)
        nc.sync.dma_start(out=sin_sb[:], in_=rope_sin.rearrange("(p j) i -> p j i", p=P))
        for load in range(1, len(LOAD_TILES)):
            load_tokens(load)

        ROTATED = 2 * PLANE
        w_grouped = const.tile([P, COLS, PACK], BF16, align_bytes=64)
        for e in range(2):
            nc.vector.tensor_copy(
                out=w_grouped[:, e * PLANE : (e + 1) * PLANE, :].rearrange("q (h i) t -> q h i t", h=HEADS),
                in_=w_raw[:].rearrange("q t (h z i e) -> q z e h i t", h=HEADS, z=2, e=2)[:, 1, 1 - e],
            )
        nc.scalar.copy(
            out=w_grouped[:, ROTATED:COLS, :].rearrange("q (h d) t -> q h d t", h=HEADS),
            in_=w_raw[:].rearrange("q t (h z d) -> q z h d t", h=HEADS, z=2)[:, 0],
        )
        w_codes = const.tile([P, COLS], U32, align_bytes=64)
        w_scales = const.tile([P, COLS], U8, align_bytes=64)

        def quantise_w(cols):
            nc.vector.quantize_mx(
                out=w_codes[:, cols].bitcast(FP8X4),
                scales=w_scales[:, cols],
                in_=w_grouped[:, cols, :].rearrange("q c t -> q (c t)"),
            )

        minus_cos = const.tile([P, TILES_PER_BATCH, PAIRS], BF16)
        member_factors = const.tile([P, TILES_PER_BATCH, PAIRS, 2], F32)
        for tiles in (slice(0, LOAD_TILES[0]), slice(LOAD_TILES[0], TILES_PER_BATCH)):
            nc.gpsimd.tensor_scalar(
                out=minus_cos[:, tiles], in0=cos_sb[:, tiles], scalar1=-1.0, scalar2=0.0, op0=MULT, op1=ADD
            )
            for e, op in ((0, SUBTRACT), (1, ADD)):
                nc.gpsimd.tensor_tensor(
                    out=member_factors[:, tiles, :, e], in0=minus_cos[:, tiles], in1=sin_sb[:, tiles], op=op
                )

        def transpose(first_step, steps):
            grouped = grouped_pool.tile([P, 2 * STEP_TILES * P * PACK], BF16, align_bytes=64)
            half = STEP_TILES * P * PACK
            for s in range(steps):
                words, first_word = step_words[first_step + s]
                xt = xt_pool.tile([P, STEP_TILES, 2, P], F32)
                for t in range(STEP_TILES):
                    start = first_word + t * WORDS
                    for u in range(2):
                        nc.tensor.transpose(xt[:, t, u, :], words[:, start + u : start + WORDS : 2], ident[:])
                nc.scalar.copy(
                    out=grouped[:, s * half : (s + 1) * half]
                    .bitcast(F32)
                    .rearrange("q (t n u) -> q t n u", t=STEP_TILES, u=2),
                    in_=xt[:].rearrange("q t u n -> q t n u"),
                )
            return grouped

        def quantise(grouped, steps):
            tokens = steps * STEP_TILES * P
            x_codes = mx_pool.tile([P, 2 * STEP_TILES * P], U32, align_bytes=64)
            x_scales = mx_pool.tile([P, 2 * STEP_TILES * P], U8, align_bytes=64)
            nc.vector.quantize_mx(
                out=x_codes[:, 0:tokens].bitcast(FP8X4),
                scales=x_scales[:, 0:tokens],
                in_=grouped[:, 0 : tokens * PACK],
            )
            return x_codes, x_scales

        def multiply(bank, x_codes, x_scales, tile, cols, start=True, stop=True):
            tokens = slice(tile * P, (tile + 1) * P)
            nc.tensor.matmul_mx(
                out=bank,
                lhsT=x_codes[:, tokens].bitcast(FP8X4),
                lhsT_scale=x_scales[:, tokens],
                rhs=w_codes[:, cols].bitcast(FP8X4),
                rhs_scale=w_scales[:, cols],
                start=start,
                stop=stop,
            )

        def scale_sums(tiles, first_tile, sums, scaled_sums):
            j0, count = (first_tile + tiles.start) % TILES_PER_BATCH, tiles.stop - tiles.start
            shape = [P, count, HEADS, PAIRS]
            nc.vector.tensor_tensor(
                out=scaled_sums[:, tiles].rearrange("p t (h i) -> p t h i", h=HEADS),
                in0=sums[:, tiles].rearrange("p t (h i) -> p t h i", h=HEADS),
                in1=cos_sb[:, j0 : j0 + count].unsqueeze(2).to_broadcast(shape),
                op=MULT,
            )

        def scale_members(tiles, first_tile, members, scaled_members):
            j0, count = (first_tile + tiles.start) % TILES_PER_BATCH, tiles.stop - tiles.start
            shape = [P, count, HEADS, PAIRS, 2]
            nc.vector.tensor_tensor(
                out=scaled_members[:, tiles].rearrange("p t (h i) e -> p t h i e", h=HEADS),
                in0=members[:].rearrange("p t e (h i) -> p t h i e", h=HEADS),
                in1=member_factors[:, j0 : j0 + count].unsqueeze(2).to_broadcast(shape),
                op=MULT,
            )

        def add(engine, tiles, scaled_sums, scaled_members, result):
            shape = [P, tiles.stop - tiles.start, HEADS, PAIRS, 2]
            engine.tensor_tensor(
                out=result[:, tiles, :, NOPE:HEAD_DIM].rearrange("p t h (i e) -> p t h i e", e=2),
                in0=scaled_sums[:, tiles]
                .rearrange("p t (h i) -> p t h i", h=HEADS)
                .unsqueeze(4)
                .to_broadcast(shape),
                in1=scaled_members[:, tiles].rearrange("p t (h i) e -> p t h i e", h=HEADS),
                op=ADD,
            )

        def store(first_tile, tiles, result):
            b, j = divmod(first_tile + tiles.start, TILES_PER_BATCH)
            nc.sync.dma_start(
                out=out_view[b, :, j : j + tiles.stop - tiles.start, :],
                in_=result[:, tiles].rearrange("p t h d -> p t (h d)"),
            )

        firsts = [sum(GROUPS[:g]) for g in range(len(GROUPS))]
        quantise_w(slice(0, ROTATED))
        staged = []
        for g in range(AHEAD):
            grouped = transpose(firsts[g], GROUPS[g])
            staged.append(quantise(grouped, GROUPS[g]))
            if g == 0:
                quantise_w(slice(ROTATED, COLS))
        first_half, second_half = slice(0, STEP_TILES), slice(STEP_TILES, 2 * STEP_TILES)
        for g in range(len(GROUPS)):
            ahead = g + AHEAD
            final = g == len(GROUPS) - 1
            if ahead < len(GROUPS):
                grouped = transpose(firsts[ahead], GROUPS[ahead])
            first_tile = firsts[g] * STEP_TILES
            halves = (first_half, second_half)[: GROUPS[g]]
            x_codes, x_scales = staged[g]

            sums = sums_pool.tile([P, 2 * STEP_TILES, PLANE], F32)
            for tile in range(GROUPS[g] * STEP_TILES):
                multiply(sums[:, tile], x_codes, x_scales, tile, slice(0, PLANE), stop=False)
                multiply(sums[:, tile], x_codes, x_scales, tile, slice(PLANE, ROTATED), start=False)
            members = []
            for half in halves:
                bank = members_pool.tile([P, STEP_TILES, 2, PLANE], F32)
                for t in range(STEP_TILES):
                    out_cols = bank[:, t].rearrange("p e c -> p (e c)")
                    multiply(out_cols, x_codes, x_scales, half.start + t, slice(0, ROTATED))
                members.append(bank)
            result = out_pool.tile([P, 2 * STEP_TILES, HEADS, HEAD_DIM], F32)
            for half in halves:
                plain = plain_pool.tile([P, STEP_TILES, PLAIN_COLS], F32)
                for t in range(STEP_TILES):
                    multiply(plain[:, t], x_codes, x_scales, half.start + t, slice(ROTATED, COLS))
                nc.scalar.copy(
                    out=result[:, half, :, 0:NOPE],
                    in_=plain[:].rearrange("p t (h d) -> p t h d", h=HEADS),
                )

            scaled_sums = product_pool.tile([P, 2 * STEP_TILES, PLANE], F32)
            scaled_members = product_pool.tile([P, 2 * STEP_TILES, PLANE, 2], F32)
            scale_sums(first_half, first_tile, sums, scaled_sums)
            for half, bank in zip(halves, members):
                scale_members(half, first_tile, bank, scaled_members)
            add(nc.vector, first_half, scaled_sums, scaled_members, result)
            if ahead < len(GROUPS):
                staged.append(quantise(grouped, GROUPS[ahead]))
            if GROUPS[g] > 1:
                scale_sums(second_half, first_tile, sums, scaled_sums)
                add(nc.vector if final else nc.gpsimd, second_half, scaled_sums, scaled_members, result)
            if final:
                for half in halves:
                    store(first_tile, half, result)
            else:
                store(first_tile, slice(0, GROUPS[g] * STEP_TILES), result)
